import numpy as np
import ml_dtypes

BF16 = ml_dtypes.bfloat16


def bf(x):
    return np.asarray(x, np.float32).astype(BF16)


def f32(x):
    return np.asarray(x, np.float32)


def f64(x):
    return np.asarray(x).astype(np.float64)


def striped(idx):
    return np.tile(idx.reshape(-1, 16).T, (8, 1))


C, S, N = 384, 512, 256


def setup_inputs():
    return {"t": f32(np.random.standard_normal((C, S))), "z_noise": f32(np.random.standard_normal((C, N))), "log_s_c": f32(0.3 * np.random.standard_normal((C, N))), "offs": striped(np.random.permutation(S)[:N])}


def reference(t, z_noise, log_s_c, offs):
    idx = offs[:16].T.reshape(-1)
    return (f64(t)[:, idx] + f64(z_noise)) * np.exp(f64(log_s_c))

@@ -1,0 +1,46 @@
+import concourse.mybir as mybir
+
+F32 = mybir.dt.float32
+U16 = mybir.dt.uint16
+ADD = mybir.AluOpType.add
+MULT = mybir.AluOpType.mult
+EXP = mybir.ActivationFunctionType.Exp
+
+P = 128
+
+
+def tile_linearcategoricalencoding_kernel(tc, t, z_noise, log_s_c, offs, out):
+    nc = tc.nc
+    channels, categories = t.shape
+    tokens = z_noise.shape[1]
+    blocks = channels // P
+
+    t_blocks = t.rearrange("(p b) s -> p b s", b=blocks)
+    log_s_c_blocks = log_s_c.rearrange("(p b) n -> p b n", b=blocks)
+    out_blocks = out.rearrange("(p b) n -> p b n", b=blocks)
+
+    with tc.tile_pool(name="held", bufs=1) as held:
+        offsets = held.tile([P, tokens // 16], U16, name="offsets")
+
+        noise = held.tile([P, blocks, tokens], F32, name="noise")
+        nc.scalar.dma_start(noise[:], z_noise.rearrange("(p b) n -> p b n", b=blocks))
+
+        tables = [held.tile([P, categories], F32, name=f"table{b}") for b in range(blocks)]
+        log_scales = [held.tile([P, tokens], F32, name=f"log_scale{b}") for b in range(blocks)]
+        for b in range(blocks):
+            nc.sync.dma_start(tables[b][:], t_blocks[:, b, :])
+            if b == 0:
+                nc.sync.dma_start(offsets[:], offs)
+        for b in range(blocks):
+            nc.sync.dma_start(log_scales[b][:], log_s_c_blocks[:, b, :])
+
+        for b in range(blocks):
+            shifted = held.tile([P, tokens], F32, name=f"shifted{b}")
+            nc.vector.tensor_tensor(shifted[:], tables[b][:].indirect(offsets[:]), noise[:, b, :], ADD)
+
+            scale = held.tile([P, tokens], F32, name=f"scale{b}")
+            nc.scalar.activation(scale[:], log_scales[b][:], EXP)
+
+            encoded = held.tile([P, tokens], F32, name=f"encoded{b}")
+            nc.vector.tensor_tensor(encoded[:], shifted[:], scale[:], MULT)
+            nc.sync.dma_start(out_blocks[:, b, :], encoded[:])

@@ -35,12 +35,16 @@ def tile_linearcategoricalencoding_kernel(tc, t, z_noise, log_s_c, offs, out):
             nc.sync.dma_start(log_scales[b][:], log_s_c_blocks[:, b, :])
 
         for b in range(blocks):
+            parts = 2 if b == blocks - 1 else 1
+            width = tokens // parts
+
             shifted = held.tile([P, tokens], F32, name=f"shifted{b}")
             nc.vector.tensor_tensor(shifted[:], tables[b][:].indirect(offsets[:]), noise[:, b, :], ADD)
 
             scale = held.tile([P, tokens], F32, name=f"scale{b}")
-            nc.scalar.activation(scale[:], log_scales[b][:], EXP)
-
             encoded = held.tile([P, tokens], F32, name=f"encoded{b}")
-            nc.vector.tensor_tensor(encoded[:], shifted[:], scale[:], MULT)
+            for part in range(parts):
+                cols = slice(part * width, (part + 1) * width)
+                nc.scalar.activation(scale[:, cols], log_scales[b][:, cols], EXP)
+                nc.vector.tensor_tensor(encoded[:, cols], shifted[:, cols], scale[:, cols], MULT)
             nc.sync.dma_start(out_blocks[:, b, :], encoded[:])

@@ -23,7 +23,10 @@ def tile_linearcategoricalencoding_kernel(tc, t, z_noise, log_s_c, offs, out):
         offsets = held.tile([P, tokens // 16], U16, name="offsets")
 
         noise = held.tile([P, blocks, tokens], F32, name="noise")
-        nc.scalar.dma_start(noise[:], z_noise.rearrange("(p b) n -> p b n", b=blocks))
+        z_noise_blocks = z_noise.rearrange("(p b) n -> p b n", b=blocks)
+        last = blocks - 1
+        nc.scalar.dma_start(noise[:, :last, :], z_noise_blocks[:, :last, :])
+        nc.scalar.dma_start(noise[:, last:, :], z_noise_blocks[:, last:, :])
 
         tables = [held.tile([P, categories], F32, name=f"table{b}") for b in range(blocks)]
         log_scales = [held.tile([P, tokens], F32, name=f"log_scale{b}") for b in range(blocks)]
@@ -35,16 +38,13 @@ def tile_linearcategoricalencoding_kernel(tc, t, z_noise, log_s_c, offs, out):
             nc.sync.dma_start(log_scales[b][:], log_s_c_blocks[:, b, :])
 
         for b in range(blocks):
-            parts = 2 if b == blocks - 1 else 1
-            width = tokens // parts
-
             shifted = held.tile([P, tokens], F32, name=f"shifted{b}")
             nc.vector.tensor_tensor(shifted[:], tables[b][:].indirect(offsets[:]), noise[:, b, :], ADD)
 
             scale = held.tile([P, tokens], F32, name=f"scale{b}")
             encoded = held.tile([P, tokens], F32, name=f"encoded{b}")
-            for part in range(parts):
-                cols = slice(part * width, (part + 1) * width)
+            half = tokens // 2
+            for cols in (slice(0, half), slice(half, tokens)):
                 nc.scalar.activation(scale[:, cols], log_scales[b][:, cols], EXP)
                 nc.vector.tensor_tensor(encoded[:, cols], shifted[:, cols], scale[:, cols], MULT)
             nc.sync.dma_start(out_blocks[:, b, :], encoded[:])

@@ -28,12 +28,11 @@ def tile_linearcategoricalencoding_kernel(tc, t, z_noise, log_s_c, offs, out):
         nc.scalar.dma_start(noise[:, :last, :], z_noise_blocks[:, :last, :])
         nc.scalar.dma_start(noise[:, last:, :], z_noise_blocks[:, last:, :])
 
+        nc.sync.dma_start(offsets[:], offs)
         tables = [held.tile([P, categories], F32, name=f"table{b}") for b in range(blocks)]
         log_scales = [held.tile([P, tokens], F32, name=f"log_scale{b}") for b in range(blocks)]
         for b in range(blocks):
             nc.sync.dma_start(tables[b][:], t_blocks[:, b, :])
-            if b == 0:
-                nc.sync.dma_start(offsets[:], offs)
         for b in range(blocks):
             nc.sync.dma_start(log_scales[b][:], log_s_c_blocks[:, b, :])
 

@@ -24,9 +24,7 @@ def tile_linearcategoricalencoding_kernel(tc, t, z_noise, log_s_c, offs, out):
 
         noise = held.tile([P, blocks, tokens], F32, name="noise")
         z_noise_blocks = z_noise.rearrange("(p b) n -> p b n", b=blocks)
-        last = blocks - 1
-        nc.scalar.dma_start(noise[:, :last, :], z_noise_blocks[:, :last, :])
-        nc.scalar.dma_start(noise[:, last:, :], z_noise_blocks[:, last:, :])
+        nc.scalar.dma_start(noise[:], z_noise_blocks)
 
         nc.sync.dma_start(offsets[:], offs)
         tables = [held.tile([P, categories], F32, name=f"table{b}") for b in range(blocks)]

import concourse.mybir as mybir

F32 = mybir.dt.float32
U16 = mybir.dt.uint16
ADD = mybir.AluOpType.add
MULT = mybir.AluOpType.mult
EXP = mybir.ActivationFunctionType.Exp

P = 128


def tile_linearcategoricalencoding_kernel(tc, t, z_noise, log_s_c, offs, out):
    nc = tc.nc
    channels, categories = t.shape
    tokens = z_noise.shape[1]
    blocks = channels // P

    t_blocks = t.rearrange("(p b) s -> p b s", b=blocks)
    log_s_c_blocks = log_s_c.rearrange("(p b) n -> p b n", b=blocks)
    out_blocks = out.rearrange("(p b) n -> p b n", b=blocks)

    with tc.tile_pool(name="held", bufs=1) as held:
        offsets = held.tile([P, tokens // 16], U16, name="offsets")

        noise = held.tile([P, blocks, tokens], F32, name="noise")
        z_noise_blocks = z_noise.rearrange("(p b) n -> p b n", b=blocks)
        nc.scalar.dma_start(noise[:], z_noise_blocks)

        nc.sync.dma_start(offsets[:], offs)
        tables = [held.tile([P, categories], F32, name=f"table{b}") for b in range(blocks)]
        log_scales = [held.tile([P, tokens], F32, name=f"log_scale{b}") for b in range(blocks)]
        for b in range(blocks):
            nc.sync.dma_start(tables[b][:], t_blocks[:, b, :])
        for b in range(blocks):
            nc.sync.dma_start(log_scales[b][:], log_s_c_blocks[:, b, :])

        for b in range(blocks):
            shifted = held.tile([P, tokens], F32, name=f"shifted{b}")
            nc.vector.tensor_tensor(shifted[:], tables[b][:].indirect(offsets[:]), noise[:, b, :], ADD)

            scale = held.tile([P, tokens], F32, name=f"scale{b}")
            encoded = held.tile([P, tokens], F32, name=f"encoded{b}")
            half = tokens // 2
            for cols in (slice(0, half), slice(half, tokens)):
                nc.scalar.activation(scale[:, cols], log_scales[b][:, cols], EXP)
                nc.vector.tensor_tensor(encoded[:, cols], shifted[:, cols], scale[:, cols], MULT)
            nc.sync.dma_start(out_blocks[:, b, :], encoded[:])
